import numpy as np
import ml_dtypes


def mxq(x, axis, fmt="e4m3"):
    dtype, down = {"e4m3": (ml_dtypes.float8_e4m3fn, 7), "e5m2": (ml_dtypes.float8_e5m2, 14)}[fmt]
    v = np.moveaxis(np.asarray(x, np.float32).astype(ml_dtypes.bfloat16).astype(np.float64), axis, -1)
    blocks = v.reshape(v.shape[:-1] + (-1, 32))
    amax = np.abs(blocks).max(-1, keepdims=True)
    byte = np.maximum(np.where(amax > 0, np.frexp(amax)[1] - 1 + 127, 0) - down, 1)
    scale = np.exp2(byte - 127.0)
    codes = (blocks / scale).astype(np.float32).astype(dtype).astype(np.float64)
    return np.moveaxis((codes * scale).reshape(v.shape), -1, axis)


WIDE = False


def mx_kscale(k):
    if not WIDE:
        return np.ones(k)
    levels = np.array([10, -10, 5, -5, 0])
    a = np.random.permutation(np.resize(levels, k // 512 * 4)).reshape(k // 512, 4)
    idx = np.arange(k)
    return np.exp2(a[idx // 512, idx % 128 // 32])


BF16 = ml_dtypes.bfloat16


def bf(x):
    return np.asarray(x, np.float32).astype(BF16)


def f64(x):
    return np.asarray(x).astype(np.float64)


E2M1 = np.array([0.0, 0.5, 1.0, 1.5, 2.0, 3.0, 4.0, 6.0, -0.0, -0.5, -1.0, -1.5, -2.0, -3.0, -4.0, -6.0])


def pack_weight(w, fmt):
    k, n = w.shape
    w = f64(bf(w)).reshape(k // 32, 32, n)
    amax = np.abs(w).max(1)
    if fmt == "e4m3":
        byte = np.frexp(amax)[1] - 1 + 127 - 7
    else:
        mant, ex = np.frexp(amax / 6.0)
        byte = np.where(mant > 0.5, ex, ex - 1) + 127
    byte = np.clip(np.where(amax > 0, byte, 1), 1, 254)
    scaled = (w * np.exp2(127.0 - byte)[:, None, :]).reshape(k, n).astype(np.float32)
    by_word = np.ascontiguousarray(scaled.reshape(k // 512, 128, 4, n).transpose(0, 1, 3, 2))
    if fmt == "e4m3":
        words = by_word.astype(ml_dtypes.float8_e4m3fn).view(np.uint8)
    else:
        c = by_word.astype(ml_dtypes.float4_e2m1fn).view(np.uint8) & 0xF
        words = c[..., 0::2] | (c[..., 1::2] << 4)
    return np.ascontiguousarray(words), np.ascontiguousarray(byte.astype(np.uint8).reshape(k // 512, 16, n))


def unpack_weight(words, scales, fmt):
    g, p, n, _ = words.shape
    if fmt == "e4m3":
        vals = np.ascontiguousarray(words).view(ml_dtypes.float8_e4m3fn).astype(np.float64)
    else:
        nib = np.empty((g, p, n, 4), np.uint8)
        nib[..., 0::2] = words & 0xF
        nib[..., 1::2] = words >> 4
        vals = E2M1[nib]
    vals = vals * np.repeat(np.exp2(scales.astype(np.float64) - 127.0), 8, axis=1)[..., None]
    return vals.transpose(0, 1, 3, 2).reshape(g * 512, n)


B, N, G, L = 1024, 512, 128, 768
N2 = 2 * N
FMT = "e4m3"


def setup_inputs():
    s = mx_kscale(N2)
    Volt = bf(np.random.standard_normal((B, N2)) * s)
    Y = np.random.standard_normal((N2, N2)) / np.sqrt(N2) / s[None, :] / s[:, None]
    Yconj = np.random.standard_normal((N2, N2)) / np.sqrt(N2) / s[None, :] / s[:, None]
    Y_words, Y_scales = pack_weight(np.ascontiguousarray(Y.T), FMT)
    Yconj_words, Yconj_scales = pack_weight(np.ascontiguousarray(Yconj.T), FMT)
    return {
        "Volt": Volt,
        "Y_words": Y_words,
        "Y_scales": Y_scales,
        "Yconj_words": Yconj_words,
        "Yconj_scales": Yconj_scales,
    }


def reference(Volt, Y_words, Y_scales, Yconj_words, Yconj_scales):
    v = f64(Volt)
    vq = mxq(v, 1, "e4m3")
    quad_p = v * (vq @ unpack_weight(Y_words, Y_scales, FMT))
    quad_q = v * (vq @ unpack_weight(Yconj_words, Yconj_scales, FMT))
    return quad_p, quad_q

@@ -1,0 +1,126 @@
+from contextlib import ExitStack
+
+import concourse.mybir as mybir
+from concourse.masks import make_identity
+
+F32 = mybir.dt.float32
+BF16 = mybir.dt.bfloat16
+I32 = mybir.dt.int32
+U32 = mybir.dt.uint32
+U8 = mybir.dt.uint8
+FP8X4 = mybir.dt.float8_e4m3fn_x4
+
+P = 128
+PACK = 4
+K_PASS = P * PACK
+BANK = 512
+QUADRANTS = 4
+ROWS = 4
+LOAD_TILES = 2
+
+FLOPS = 2 * 2 * 1024 * 1024 * 1024
+
+
+def tile_pinnlayer_pb_kernel(
+    tc, Volt, Y_words, Y_scales, Yconj_words, Yconj_scales, out_0, out_1
+):
+    nc = tc.nc
+    samples, width = Volt.shape
+    row_tiles = samples // P
+    passes = width // K_PASS
+    banks = width // BANK
+    words_in = (Y_words, Yconj_words)
+    scales_in = (Y_scales, Yconj_scales)
+    outs = (out_0, out_1)
+
+    volt_rows = Volt.rearrange("(p t) k -> p t k", t=row_tiles)
+    out_rows = [o.rearrange("(p t) n -> p t n", t=row_tiles) for o in outs]
+
+    with ExitStack() as ctx:
+        keep = ctx.enter_context(tc.tile_pool(name="keep", bufs=1))
+        stage = ctx.enter_context(tc.tile_pool(name="stage", bufs=3))
+        results = ctx.enter_context(tc.tile_pool(name="results", bufs=6))
+        psum = ctx.enter_context(tc.psum_pool(name="psum", bufs=8))
+
+        identity = keep.tile([P, P], F32)
+        volt = keep.tile([P, row_tiles, width], BF16)
+        w_words = keep.tile([P, len(outs), passes, width], U32, align_bytes=64)
+        w_planes = keep.tile([P, width], U8, align_bytes=64)
+        v_words = keep.tile([P, row_tiles, passes, P], U32, align_bytes=64)
+        v_planes = keep.tile([P, row_tiles, passes, P], U8, align_bytes=64)
+
+        make_identity(nc, identity[:])
+        nc.vector.memset(w_planes[:].bitcast(I32), 0)
+
+        def load_volt(first):
+            tiles = slice(first, first + LOAD_TILES)
+            nc.sync.dma_start(out=volt[:, tiles, :], in_=volt_rows[:, tiles, :])
+
+        def load_scales(w):
+            for quadrant in range(QUADRANTS):
+                first = 32 * quadrant + ROWS * passes * w
+                nc.sync.dma_start(
+                    out=w_planes[first : first + ROWS * passes, :].bitcast(I32),
+                    in_=scales_in[w][:, ROWS * quadrant : ROWS * (quadrant + 1), :].bitcast(I32),
+                )
+
+        def load_words(w):
+            for g in range(passes):
+                nc.sync.dma_start(
+                    out=w_words[:, w, g, :].bitcast(I32),
+                    in_=words_in[w][g].rearrange("p n t4 -> p (n t4)").bitcast(I32),
+                )
+
+        load_volt(0)
+        load_volt(2)
+        load_scales(0)
+        load_volt(4)
+        load_volt(6)
+        load_words(0)
+        load_scales(1)
+        load_words(1)
+
+        for t in range(row_tiles):
+            pairs = volt[:, t, :].bitcast(F32)
+            flipped = psum.tile([P, passes, 2, P], F32, tag="bank")
+            for g in range(passes):
+                for u in range(2):
+                    first = (K_PASS // 2) * g + u
+                    nc.tensor.transpose(
+                        flipped[:, g, u, :],
+                        pairs[:, first : (K_PASS // 2) * (g + 1) : 2],
+                        identity[:],
+                    )
+            grouped = stage.tile([P, passes, P, PACK], BF16, align_bytes=64)
+            nc.scalar.copy(
+                out=grouped[:]
+                .rearrange("p g b t4 -> p (g b t4)")
+                .bitcast(F32)
+                .rearrange("p (g b u) -> p g b u", g=passes, u=2),
+                in_=flipped[:].rearrange("p g u b -> p g b u"),
+            )
+            nc.vector.quantize_mx(
+                out=v_words[:, t, :, :].rearrange("p g b -> p (g b)").bitcast(FP8X4),
+                scales=v_planes[:, t, :, :].rearrange("p g b -> p (g b)"),
+                in_=grouped[:].rearrange("p g b t4 -> p (g b t4)"),
+            )
+
+        for w in range(len(outs)):
+            for t in range(row_tiles):
+                product = results.tile([P, width], F32)
+                for c in range(banks):
+                    n_cols = slice(BANK * c, BANK * (c + 1))
+                    acc = psum.tile([P, BANK], F32, tag="bank")
+                    for g in range(passes):
+                        plane_first = ROWS * (passes * w + g)
+                        nc.tensor.matmul_mx(
+                            out=acc[:],
+                            lhsT=v_words[:, t, g, :].bitcast(FP8X4),
+                            lhsT_scale=v_planes[:, t, g, :],
+                            rhs=w_words[:, w, g, n_cols].bitcast(FP8X4),
+                            rhs_scale=w_planes[plane_first:P, n_cols],
+                            start=(g == 0),
+                            stop=(g == passes - 1),
+                        )
+                    nc.vector.tensor_mul(product[:, n_cols], acc[:], volt[:, t, n_cols])
+                nc.sync.dma_start(out=out_rows[w][:, t, :], in_=product[:])

@@ -17,6 +17,7 @@ BANK = 512
 QUADRANTS = 4
 ROWS = 4
 LOAD_TILES = 2
+SHARE = 4
 
 FLOPS = 2 * 2 * 1024 * 1024 * 1024
 
@@ -122,5 +123,11 @@ def tile_pinnlayer_pb_kernel(
                             start=(g == 0),
                             stop=(g == passes - 1),
                         )
-                    nc.vector.tensor_mul(product[:, n_cols], acc[:], volt[:, t, n_cols])
+                    if (banks * t + c) % SHARE == 0:
+                        nc.scalar.copy(out=product[:, n_cols], in_=acc[:])
+                        nc.gpsimd.tensor_mul(
+                            product[:, n_cols], product[:, n_cols], volt[:, t, n_cols]
+                        )
+                    else:
+                        nc.vector.tensor_mul(product[:, n_cols], acc[:], volt[:, t, n_cols])
                 nc.sync.dma_start(out=out_rows[w][:, t, :], in_=product[:])

@@ -17,7 +17,6 @@ BANK = 512
 QUADRANTS = 4
 ROWS = 4
 LOAD_TILES = 2
-SHARE = 4
 
 FLOPS = 2 * 2 * 1024 * 1024 * 1024
 
@@ -42,6 +41,7 @@ def tile_pinnlayer_pb_kernel(
         stage = ctx.enter_context(tc.tile_pool(name="stage", bufs=3))
         results = ctx.enter_context(tc.tile_pool(name="results", bufs=6))
         psum = ctx.enter_context(tc.psum_pool(name="psum", bufs=8))
+        ctx.enter_context(tc.manual_schedule())
 
         identity = keep.tile([P, P], F32)
         volt = keep.tile([P, row_tiles, width], BF16)
@@ -123,11 +123,5 @@ def tile_pinnlayer_pb_kernel(
                             start=(g == 0),
                             stop=(g == passes - 1),
                         )
-                    if (banks * t + c) % SHARE == 0:
-                        nc.scalar.copy(out=product[:, n_cols], in_=acc[:])
-                        nc.gpsimd.tensor_mul(
-                            product[:, n_cols], product[:, n_cols], volt[:, t, n_cols]
-                        )
-                    else:
-                        nc.vector.tensor_mul(product[:, n_cols], acc[:], volt[:, t, n_cols])
+                    nc.vector.tensor_mul(product[:, n_cols], acc[:], volt[:, t, n_cols])
                 nc.sync.dma_start(out=out_rows[w][:, t, :], in_=product[:])

@@ -51,6 +51,14 @@ def tile_pinnlayer_pb_kernel(
         v_planes = keep.tile([P, row_tiles, passes, P], U8, align_bytes=64)
 
         make_identity(nc, identity[:])
+        zeros = keep.tile([P, BANK], BF16)
+        nc.gpsimd.memset(zeros[:], 0.0)
+
+        def idle_matmuls(count):
+            unread = psum.tile([P, BANK], F32, tag="bank")
+            for i in range(count):
+                nc.tensor.matmul(unread[:], lhsT=zeros[:, 0:P], rhs=zeros[:], start=True, stop=True)
+
         nc.vector.memset(w_planes[:].bitcast(I32), 0)
 
         def load_volt(first):
@@ -81,7 +89,10 @@ def tile_pinnlayer_pb_kernel(
         load_scales(1)
         load_words(1)
 
+        idle_matmuls(6)
         for t in range(row_tiles):
+            if t > 0 and t % 2 == 0:
+                idle_matmuls(2)
             pairs = volt[:, t, :].bitcast(F32)
             flipped = psum.tile([P, passes, 2, P], F32, tag="bank")
             for g in range(passes):

@@ -38,27 +38,21 @@ def tile_pinnlayer_pb_kernel(
 
     with ExitStack() as ctx:
         keep = ctx.enter_context(tc.tile_pool(name="keep", bufs=1))
-        stage = ctx.enter_context(tc.tile_pool(name="stage", bufs=3))
-        results = ctx.enter_context(tc.tile_pool(name="results", bufs=6))
+        stage = ctx.enter_context(tc.tile_pool(name="stage", bufs=row_tiles))
+        results = ctx.enter_context(tc.tile_pool(name="results", bufs=len(outs) * row_tiles))
         psum = ctx.enter_context(tc.psum_pool(name="psum", bufs=8))
         ctx.enter_context(tc.manual_schedule())
 
         identity = keep.tile([P, P], F32)
+        zeros = keep.tile([P, BANK], BF16)
         volt = keep.tile([P, row_tiles, width], BF16)
         w_words = keep.tile([P, len(outs), passes, width], U32, align_bytes=64)
         w_planes = keep.tile([P, width], U8, align_bytes=64)
         v_words = keep.tile([P, row_tiles, passes, P], U32, align_bytes=64)
         v_planes = keep.tile([P, row_tiles, passes, P], U8, align_bytes=64)
 
-        make_identity(nc, identity[:])
-        zeros = keep.tile([P, BANK], BF16)
         nc.gpsimd.memset(zeros[:], 0.0)
-
-        def idle_matmuls(count):
-            unread = psum.tile([P, BANK], F32, tag="bank")
-            for i in range(count):
-                nc.tensor.matmul(unread[:], lhsT=zeros[:, 0:P], rhs=zeros[:], start=True, stop=True)
-
+        make_identity(nc, identity[:])
         nc.vector.memset(w_planes[:].bitcast(I32), 0)
 
         def load_volt(first):
@@ -73,26 +67,33 @@ def tile_pinnlayer_pb_kernel(
                     in_=scales_in[w][:, ROWS * quadrant : ROWS * (quadrant + 1), :].bitcast(I32),
                 )
 
-        def load_words(w):
-            for g in range(passes):
-                nc.sync.dma_start(
-                    out=w_words[:, w, g, :].bitcast(I32),
-                    in_=words_in[w][g].rearrange("p n t4 -> p (n t4)").bitcast(I32),
-                )
+        def load_words(w, c):
+            n_cols = slice(BANK * c, BANK * (c + 1))
+            byte_cols = slice(PACK * BANK * c, PACK * BANK * (c + 1))
+            nc.sync.dma_start(
+                out=w_words[:, w, :, n_cols].bitcast(I32),
+                in_=words_in[w].rearrange("g p n t4 -> p g (n t4)")[:, :, byte_cols].bitcast(I32),
+            )
 
         load_volt(0)
-        load_volt(2)
         load_scales(0)
+        load_words(0, 0)
+        load_words(0, 1)
+        load_volt(2)
         load_volt(4)
         load_volt(6)
-        load_words(0)
         load_scales(1)
-        load_words(1)
+        load_words(1, 0)
+        load_words(1, 1)
 
-        idle_matmuls(6)
-        for t in range(row_tiles):
-            if t > 0 and t % 2 == 0:
-                idle_matmuls(2)
+        def idle_matmuls(count):
+            unread = psum.tile([P, BANK], F32, tag="bank")
+            for i in range(count):
+                nc.tensor.matmul(unread[:], lhsT=zeros[:, 0:P], rhs=zeros[:], start=True, stop=True)
+
+        grouped_of = {}
+
+        def flip(t):
             pairs = volt[:, t, :].bitcast(F32)
             flipped = psum.tile([P, passes, 2, P], F32, tag="bank")
             for g in range(passes):
@@ -111,28 +112,68 @@ def tile_pinnlayer_pb_kernel(
                 .rearrange("p (g b u) -> p g b u", g=passes, u=2),
                 in_=flipped[:].rearrange("p g u b -> p g b u"),
             )
+            grouped_of[t] = grouped
+
+        def quantise(t):
             nc.vector.quantize_mx(
                 out=v_words[:, t, :, :].rearrange("p g b -> p (g b)").bitcast(FP8X4),
                 scales=v_planes[:, t, :, :].rearrange("p g b -> p (g b)"),
-                in_=grouped[:].rearrange("p g b t4 -> p (g b t4)"),
+                in_=grouped_of[t][:].rearrange("p g b t4 -> p (g b t4)"),
             )
 
-        for w in range(len(outs)):
-            for t in range(row_tiles):
+        product_of = {}
+
+        def multiply(w, t, c):
+            if c == 0:
                 product = results.tile([P, width], F32)
-                for c in range(banks):
-                    n_cols = slice(BANK * c, BANK * (c + 1))
-                    acc = psum.tile([P, BANK], F32, tag="bank")
-                    for g in range(passes):
-                        plane_first = ROWS * (passes * w + g)
-                        nc.tensor.matmul_mx(
-                            out=acc[:],
-                            lhsT=v_words[:, t, g, :].bitcast(FP8X4),
-                            lhsT_scale=v_planes[:, t, g, :],
-                            rhs=w_words[:, w, g, n_cols].bitcast(FP8X4),
-                            rhs_scale=w_planes[plane_first:P, n_cols],
-                            start=(g == 0),
-                            stop=(g == passes - 1),
-                        )
-                    nc.vector.tensor_mul(product[:, n_cols], acc[:], volt[:, t, n_cols])
-                nc.sync.dma_start(out=out_rows[w][:, t, :], in_=product[:])
+                product_of[(w, t)] = product
+            n_cols = slice(BANK * c, BANK * (c + 1))
+            acc = psum.tile([P, BANK], F32, tag="bank")
+            for g in range(passes):
+                plane_first = ROWS * (passes * w + g)
+                nc.tensor.matmul_mx(
+                    out=acc[:],
+                    lhsT=v_words[:, t, g, :].bitcast(FP8X4),
+                    lhsT_scale=v_planes[:, t, g, :],
+                    rhs=w_words[:, w, g, n_cols].bitcast(FP8X4),
+                    rhs_scale=w_planes[plane_first:P, n_cols],
+                    start=(g == 0),
+                    stop=(g == passes - 1),
+                )
+            nc.vector.tensor_mul(product_of[(w, t)][:, n_cols], acc[:], volt[:, t, n_cols])
+            if c == banks - 1:
+                nc.sync.dma_start(out=out_rows[w][:, t, :], in_=product_of[(w, t)][:])
+
+        def multiply_tile(w, t):
+            for c in range(banks):
+                multiply(w, t, c)
+
+        idle_matmuls(6)
+        flip(0)
+        flip(1)
+        quantise(0)
+        quantise(1)
+        multiply(0, 0, 0)
+        multiply(0, 1, 0)
+        multiply(0, 0, 1)
+        multiply(0, 1, 1)
+        flip(2)
+        flip(3)
+        flip(4)
+        flip(5)
+        quantise(2)
+        quantise(3)
+        multiply_tile(0, 2)
+        quantise(4)
+        multiply_tile(0, 3)
+        quantise(5)
+        flip(6)
+        flip(7)
+        multiply_tile(0, 4)
+        quantise(6)
+        multiply_tile(0, 5)
+        quantise(7)
+        multiply_tile(0, 6)
+        multiply_tile(0, 7)
+        for t in range(row_tiles):
+            multiply_tile(1, t)

@@ -47,13 +47,16 @@ def tile_pinnlayer_pb_kernel(
         zeros = keep.tile([P, BANK], BF16)
         volt = keep.tile([P, row_tiles, width], BF16)
         w_words = keep.tile([P, len(outs), passes, width], U32, align_bytes=64)
-        w_planes = keep.tile([P, width], U8, align_bytes=64)
+        y_planes = keep.tile([P, width], U8, align_bytes=64)
+        yconj_planes = keep.tile([P, width], U8, align_bytes=64)
+        w_planes = (y_planes, yconj_planes)
         v_words = keep.tile([P, row_tiles, passes, P], U32, align_bytes=64)
         v_planes = keep.tile([P, row_tiles, passes, P], U8, align_bytes=64)
 
         nc.gpsimd.memset(zeros[:], 0.0)
         make_identity(nc, identity[:])
-        nc.vector.memset(w_planes[:].bitcast(I32), 0)
+        nc.vector.memset(y_planes[:].bitcast(I32), 0)
+        nc.vector.memset(yconj_planes[:].bitcast(I32), 0)
 
         def load_volt(first):
             tiles = slice(first, first + LOAD_TILES)
@@ -61,9 +64,9 @@ def tile_pinnlayer_pb_kernel(
 
         def load_scales(w):
             for quadrant in range(QUADRANTS):
-                first = 32 * quadrant + ROWS * passes * w
+                first = 32 * quadrant
                 nc.sync.dma_start(
-                    out=w_planes[first : first + ROWS * passes, :].bitcast(I32),
+                    out=w_planes[w][first : first + ROWS * passes, :].bitcast(I32),
                     in_=scales_in[w][:, ROWS * quadrant : ROWS * (quadrant + 1), :].bitcast(I32),
                 )
 
@@ -130,13 +133,13 @@ def tile_pinnlayer_pb_kernel(
             n_cols = slice(BANK * c, BANK * (c + 1))
             acc = psum.tile([P, BANK], F32, tag="bank")
             for g in range(passes):
-                plane_first = ROWS * (passes * w + g)
+                plane_first = ROWS * g
                 nc.tensor.matmul_mx(
                     out=acc[:],
                     lhsT=v_words[:, t, g, :].bitcast(FP8X4),
                     lhsT_scale=v_planes[:, t, g, :],
                     rhs=w_words[:, w, g, n_cols].bitcast(FP8X4),
-                    rhs_scale=w_planes[plane_first:P, n_cols],
+                    rhs_scale=w_planes[w][plane_first:P, n_cols],
                     start=(g == 0),
                     stop=(g == passes - 1),
                 )

@@ -79,10 +79,10 @@ def tile_pinnlayer_pb_kernel(
             )
 
         load_volt(0)
+        load_volt(2)
         load_scales(0)
         load_words(0, 0)
         load_words(0, 1)
-        load_volt(2)
         load_volt(4)
         load_volt(6)
         load_scales(1)
@@ -152,31 +152,23 @@ def tile_pinnlayer_pb_kernel(
                 multiply(w, t, c)
 
         idle_matmuls(6)
-        flip(0)
-        flip(1)
-        quantise(0)
-        quantise(1)
-        multiply(0, 0, 0)
-        multiply(0, 1, 0)
-        multiply(0, 0, 1)
-        multiply(0, 1, 1)
-        flip(2)
-        flip(3)
-        flip(4)
-        flip(5)
-        quantise(2)
-        quantise(3)
-        multiply_tile(0, 2)
-        quantise(4)
-        multiply_tile(0, 3)
-        quantise(5)
-        flip(6)
-        flip(7)
-        multiply_tile(0, 4)
-        quantise(6)
-        multiply_tile(0, 5)
-        quantise(7)
-        multiply_tile(0, 6)
-        multiply_tile(0, 7)
+        half = row_tiles // 2
+        for t in range(half):
+            flip(t)
+        for t in range(half):
+            quantise(t)
+        for c in range(banks):
+            for t in range(half):
+                multiply(0, t, c)
+        for t in range(half, row_tiles):
+            flip(t)
+        quantise(half)
+        quantise(half + 1)
+        multiply_tile(0, half)
+        quantise(half + 2)
+        multiply_tile(0, half + 1)
+        quantise(half + 3)
+        multiply_tile(0, half + 2)
+        multiply_tile(0, half + 3)
         for t in range(row_tiles):
             multiply_tile(1, t)

@@ -96,17 +96,25 @@ def tile_pinnlayer_pb_kernel(
 
         grouped_of = {}
 
+        sorted_of = {}
+
+        def sort_words(t):
+            pairs = volt[:, t, :].bitcast(F32).rearrange("p (g j u) -> p g u j", g=passes, u=2)
+            in_order = stage.tile([P, passes, 2, P], F32)
+            nc.scalar.copy(out=in_order[:], in_=pairs)
+            sorted_of[t] = in_order
+
         def flip(t):
             pairs = volt[:, t, :].bitcast(F32)
             flipped = psum.tile([P, passes, 2, P], F32, tag="bank")
             for g in range(passes):
                 for u in range(2):
-                    first = (K_PASS // 2) * g + u
-                    nc.tensor.transpose(
-                        flipped[:, g, u, :],
-                        pairs[:, first : (K_PASS // 2) * (g + 1) : 2],
-                        identity[:],
-                    )
+                    if t in sorted_of:
+                        words = sorted_of[t][:, g, u, :]
+                    else:
+                        first = (K_PASS // 2) * g + u
+                        words = pairs[:, first : (K_PASS // 2) * (g + 1) : 2]
+                    nc.tensor.transpose(flipped[:, g, u, :], words, identity[:])
             grouped = stage.tile([P, passes, P, PACK], BF16, align_bytes=64)
             nc.scalar.copy(
                 out=grouped[:]
@@ -157,6 +165,8 @@ def tile_pinnlayer_pb_kernel(
             flip(t)
         for t in range(half):
             quantise(t)
+        for t in range(half, row_tiles):
+            sort_words(t)
         for c in range(banks):
             for t in range(half):
                 multiply(0, t, c)

@@ -167,12 +167,14 @@ def tile_pinnlayer_pb_kernel(
             quantise(t)
         for t in range(half, row_tiles):
             sort_words(t)
-        for c in range(banks):
-            for t in range(half):
-                multiply(0, t, c)
+        for t in range(half):
+            multiply(0, t, 0)
+        for t in range(half - 1):
+            multiply(0, t, 1)
         for t in range(half, row_tiles):
             flip(t)
         quantise(half)
+        multiply(0, half - 1, 1)
         quantise(half + 1)
         multiply_tile(0, half)
         quantise(half + 2)

@@ -167,10 +167,11 @@ def tile_pinnlayer_pb_kernel(
             quantise(t)
         for t in range(half, row_tiles):
             sort_words(t)
-        for t in range(half):
-            multiply(0, t, 0)
-        for t in range(half - 1):
-            multiply(0, t, 1)
+        for c in range(banks):
+            for t in range(half - 2):
+                multiply(0, t, c)
+        multiply_tile(0, half - 2)
+        multiply(0, half - 1, 0)
         for t in range(half, row_tiles):
             flip(t)
         quantise(half)

@@ -16,6 +16,7 @@ K_PASS = P * PACK
 BANK = 512
 QUADRANTS = 4
 ROWS = 4
+PLANE_FIRST = (0, 4)
 LOAD_TILES = 2
 
 FLOPS = 2 * 2 * 1024 * 1024 * 1024
@@ -47,27 +48,28 @@ def tile_pinnlayer_pb_kernel(
         zeros = keep.tile([P, BANK], BF16)
         volt = keep.tile([P, row_tiles, width], BF16)
         w_words = keep.tile([P, len(outs), passes, width], U32, align_bytes=64)
-        y_planes = keep.tile([P, width], U8, align_bytes=64)
-        yconj_planes = keep.tile([P, width], U8, align_bytes=64)
+        y_planes = keep.tile([P, passes, width], U8, align_bytes=64)
+        yconj_planes = keep.tile([P, passes, width], U8, align_bytes=64)
         w_planes = (y_planes, yconj_planes)
         v_words = keep.tile([P, row_tiles, passes, P], U32, align_bytes=64)
         v_planes = keep.tile([P, row_tiles, passes, P], U8, align_bytes=64)
 
-        nc.gpsimd.memset(zeros[:], 0.0)
+        nc.vector.memset(zeros[:], 0.0)
         make_identity(nc, identity[:])
-        nc.vector.memset(y_planes[:].bitcast(I32), 0)
-        nc.vector.memset(yconj_planes[:].bitcast(I32), 0)
+        for planes in w_planes:
+            nc.vector.memset(planes[:].rearrange("p g n -> p (g n)").bitcast(I32), 0)
 
         def load_volt(first):
             tiles = slice(first, first + LOAD_TILES)
             nc.sync.dma_start(out=volt[:, tiles, :], in_=volt_rows[:, tiles, :])
 
         def load_scales(w):
+            by_row = scales_in[w].rearrange("g q n -> q g n")
             for quadrant in range(QUADRANTS):
-                first = 32 * quadrant
+                first = 32 * quadrant + PLANE_FIRST[w]
                 nc.sync.dma_start(
-                    out=w_planes[w][first : first + ROWS * passes, :].bitcast(I32),
-                    in_=scales_in[w][:, ROWS * quadrant : ROWS * (quadrant + 1), :].bitcast(I32),
+                    out=w_planes[w][first : first + ROWS, :, :].bitcast(I32),
+                    in_=by_row[ROWS * quadrant : ROWS * (quadrant + 1), :, :].bitcast(I32),
                 )
 
         def load_words(w, c):
@@ -141,13 +143,12 @@ def tile_pinnlayer_pb_kernel(
             n_cols = slice(BANK * c, BANK * (c + 1))
             acc = psum.tile([P, BANK], F32, tag="bank")
             for g in range(passes):
-                plane_first = ROWS * g
                 nc.tensor.matmul_mx(
                     out=acc[:],
                     lhsT=v_words[:, t, g, :].bitcast(FP8X4),
                     lhsT_scale=v_planes[:, t, g, :],
                     rhs=w_words[:, w, g, n_cols].bitcast(FP8X4),
-                    rhs_scale=w_planes[w][plane_first:P, n_cols],
+                    rhs_scale=w_planes[w][PLANE_FIRST[w] : P, g, n_cols],
                     start=(g == 0),
                     stop=(g == passes - 1),
                 )
@@ -159,7 +160,7 @@ def tile_pinnlayer_pb_kernel(
             for c in range(banks):
                 multiply(w, t, c)
 
-        idle_matmuls(6)
+        idle_matmuls(5)
         half = row_tiles // 2
         for t in range(half):
             flip(t)
@@ -175,13 +176,13 @@ def tile_pinnlayer_pb_kernel(
         for t in range(half, row_tiles):
             flip(t)
         quantise(half)
-        multiply(0, half - 1, 1)
         quantise(half + 1)
-        multiply_tile(0, half)
+        multiply(0, half - 1, 1)
         quantise(half + 2)
-        multiply_tile(0, half + 1)
+        multiply(0, half, 0)
         quantise(half + 3)
-        multiply_tile(0, half + 2)
-        multiply_tile(0, half + 3)
+        multiply(0, half, 1)
+        for t in range(half + 1, row_tiles):
+            multiply_tile(0, t)
         for t in range(row_tiles):
             multiply_tile(1, t)

@@ -40,7 +40,7 @@ def tile_pinnlayer_pb_kernel(
     with ExitStack() as ctx:
         keep = ctx.enter_context(tc.tile_pool(name="keep", bufs=1))
         stage = ctx.enter_context(tc.tile_pool(name="stage", bufs=row_tiles))
-        results = ctx.enter_context(tc.tile_pool(name="results", bufs=len(outs) * row_tiles))
+        results = ctx.enter_context(tc.tile_pool(name="results", bufs=len(outs) * row_tiles - 2))
         psum = ctx.enter_context(tc.psum_pool(name="psum", bufs=8))
         ctx.enter_context(tc.manual_schedule())
 
@@ -72,9 +72,9 @@ def tile_pinnlayer_pb_kernel(
                     in_=by_row[ROWS * quadrant : ROWS * (quadrant + 1), :, :].bitcast(I32),
                 )
 
-        def load_words(w, c):
-            n_cols = slice(BANK * c, BANK * (c + 1))
-            byte_cols = slice(PACK * BANK * c, PACK * BANK * (c + 1))
+        def load_words(w, first, count):
+            n_cols = slice(first, first + count)
+            byte_cols = slice(PACK * first, PACK * (first + count))
             nc.sync.dma_start(
                 out=w_words[:, w, :, n_cols].bitcast(I32),
                 in_=words_in[w].rearrange("g p n t4 -> p g (n t4)")[:, :, byte_cols].bitcast(I32),
@@ -83,13 +83,12 @@ def tile_pinnlayer_pb_kernel(
         load_volt(0)
         load_volt(2)
         load_scales(0)
-        load_words(0, 0)
-        load_words(0, 1)
+        load_words(0, 0, BANK)
+        load_words(0, BANK, BANK)
         load_volt(4)
         load_volt(6)
         load_scales(1)
-        load_words(1, 0)
-        load_words(1, 1)
+        load_words(1, 0, width)
 
         def idle_matmuls(count):
             unread = psum.tile([P, BANK], F32, tag="bank")
@@ -134,12 +133,15 @@ def tile_pinnlayer_pb_kernel(
                 in_=grouped_of[t][:].rearrange("p g b t4 -> p (g b t4)"),
             )
 
+        first_two = keep.tile([P, 2, width], F32)
         product_of = {}
 
         def multiply(w, t, c):
-            if c == 0:
+            if w == 0 and t < 2:
+                product_of[(w, t)] = first_two[:, t, :]
+            elif c == 0:
                 product = results.tile([P, width], F32)
-                product_of[(w, t)] = product
+                product_of[(w, t)] = product[:]
             n_cols = slice(BANK * c, BANK * (c + 1))
             acc = psum.tile([P, BANK], F32, tag="bank")
             for g in range(passes):
@@ -153,8 +155,11 @@ def tile_pinnlayer_pb_kernel(
                     stop=(g == passes - 1),
                 )
             nc.vector.tensor_mul(product_of[(w, t)][:, n_cols], acc[:], volt[:, t, n_cols])
-            if c == banks - 1:
-                nc.sync.dma_start(out=out_rows[w][:, t, :], in_=product_of[(w, t)][:])
+            if w == 0 and t < 2:
+                if t == 1 and c == banks - 1:
+                    nc.sync.dma_start(out=out_rows[w][:, 0:2, :], in_=first_two[:])
+            elif c == banks - 1:
+                nc.sync.dma_start(out=out_rows[w][:, t, :], in_=product_of[(w, t)])
 
         def multiply_tile(w, t):
             for c in range(banks):

@@ -54,7 +54,7 @@ def tile_pinnlayer_pb_kernel(
         v_words = keep.tile([P, row_tiles, passes, P], U32, align_bytes=64)
         v_planes = keep.tile([P, row_tiles, passes, P], U8, align_bytes=64)
 
-        nc.vector.memset(zeros[:], 0.0)
+        nc.vector.memset(zeros[:].bitcast(I32), 0)
         make_identity(nc, identity[:])
         for planes in w_planes:
             nc.vector.memset(planes[:].rearrange("p g n -> p (g n)").bitcast(I32), 0)
@@ -165,9 +165,12 @@ def tile_pinnlayer_pb_kernel(
             for c in range(banks):
                 multiply(w, t, c)
 
-        idle_matmuls(5)
+        idle_matmuls(4)
         half = row_tiles // 2
-        for t in range(half):
+        for t in range(LOAD_TILES):
+            flip(t)
+        idle_matmuls(2)
+        for t in range(LOAD_TILES, half):
             flip(t)
         for t in range(half):
             quantise(t)

@@ -17,6 +17,7 @@ BANK = 512
 QUADRANTS = 4
 ROWS = 4
 PLANE_FIRST = (0, 4)
+PAIRED_STORES = 3
 LOAD_TILES = 2
 
 FLOPS = 2 * 2 * 1024 * 1024 * 1024
@@ -40,7 +41,10 @@ def tile_pinnlayer_pb_kernel(
     with ExitStack() as ctx:
         keep = ctx.enter_context(tc.tile_pool(name="keep", bufs=1))
         stage = ctx.enter_context(tc.tile_pool(name="stage", bufs=row_tiles))
-        results = ctx.enter_context(tc.tile_pool(name="results", bufs=len(outs) * row_tiles - 2))
+        results = ctx.enter_context(
+            tc.tile_pool(name="results", bufs=len(outs) * row_tiles - 2 * PAIRED_STORES)
+        )
+        pairs = ctx.enter_context(tc.tile_pool(name="pairs", bufs=PAIRED_STORES))
         psum = ctx.enter_context(tc.psum_pool(name="psum", bufs=8))
         ctx.enter_context(tc.manual_schedule())
 
@@ -80,15 +84,26 @@ def tile_pinnlayer_pb_kernel(
                 in_=words_in[w].rearrange("g p n t4 -> p g (n t4)")[:, :, byte_cols].bitcast(I32),
             )
 
+        def load_words_of_pass(w, g, first, count):
+            byte_cols = slice(PACK * first, PACK * (first + count))
+            nc.sync.dma_start(
+                out=w_words[:, w, g, first : first + count].bitcast(I32),
+                in_=words_in[w][g, :, :, :]
+                .rearrange("p n t4 -> p (n t4)")[:, byte_cols]
+                .bitcast(I32),
+            )
+
         load_volt(0)
         load_volt(2)
         load_scales(0)
-        load_words(0, 0, BANK)
+        for g in range(passes):
+            load_words_of_pass(0, g, 0, BANK)
         load_words(0, BANK, BANK)
+        load_scales(1)
+        load_words(1, 0, BANK)
+        load_words(1, BANK, BANK)
         load_volt(4)
         load_volt(6)
-        load_scales(1)
-        load_words(1, 0, width)
 
         def idle_matmuls(count):
             unread = psum.tile([P, BANK], F32, tag="bank")
@@ -133,64 +148,91 @@ def tile_pinnlayer_pb_kernel(
                 in_=grouped_of[t][:].rearrange("p g b t4 -> p (g b t4)"),
             )
 
-        first_two = keep.tile([P, 2, width], F32)
+        half = row_tiles // 2
+        paired = [(w, t) for w in range(len(outs)) for t in range(half)][: 2 * PAIRED_STORES]
+        pair_of = {}
         product_of = {}
 
-        def multiply(w, t, c):
-            if w == 0 and t < 2:
-                product_of[(w, t)] = first_two[:, t, :]
-            elif c == 0:
+        def new_product(w, t):
+            if (w, t) not in paired:
                 product = results.tile([P, width], F32)
                 product_of[(w, t)] = product[:]
+            else:
+                if t % 2 == 0:
+                    pair = pairs.tile([P, 2, width], F32)
+                    pair_of[(w, t // 2)] = pair
+                product_of[(w, t)] = pair_of[(w, t // 2)][:, t % 2, :]
+
+        def store(w, t):
+            if (w, t) not in paired:
+                nc.sync.dma_start(out=out_rows[w][:, t, :], in_=product_of[(w, t)])
+            elif t % 2 == 1:
+                nc.sync.dma_start(out=out_rows[w][:, t - 1 : t + 1, :], in_=pair_of[(w, t // 2)][:])
+
+        def add_pass(acc, w, t, c, g):
             n_cols = slice(BANK * c, BANK * (c + 1))
+            nc.tensor.matmul_mx(
+                out=acc[:],
+                lhsT=v_words[:, t, g, :].bitcast(FP8X4),
+                lhsT_scale=v_planes[:, t, g, :],
+                rhs=w_words[:, w, g, n_cols].bitcast(FP8X4),
+                rhs_scale=w_planes[w][PLANE_FIRST[w] : P, g, n_cols],
+                start=(g == 0),
+                stop=(g == passes - 1),
+            )
+
+        def finish(acc, w, t, c):
+            if c == 0:
+                new_product(w, t)
+            n_cols = slice(BANK * c, BANK * (c + 1))
+            nc.vector.tensor_mul(product_of[(w, t)][:, n_cols], acc[:], volt[:, t, n_cols])
+            if c == banks - 1:
+                store(w, t)
+
+        def multiply(w, t, c):
             acc = psum.tile([P, BANK], F32, tag="bank")
             for g in range(passes):
-                nc.tensor.matmul_mx(
-                    out=acc[:],
-                    lhsT=v_words[:, t, g, :].bitcast(FP8X4),
-                    lhsT_scale=v_planes[:, t, g, :],
-                    rhs=w_words[:, w, g, n_cols].bitcast(FP8X4),
-                    rhs_scale=w_planes[w][PLANE_FIRST[w] : P, g, n_cols],
-                    start=(g == 0),
-                    stop=(g == passes - 1),
-                )
-            nc.vector.tensor_mul(product_of[(w, t)][:, n_cols], acc[:], volt[:, t, n_cols])
-            if w == 0 and t < 2:
-                if t == 1 and c == banks - 1:
-                    nc.sync.dma_start(out=out_rows[w][:, 0:2, :], in_=first_two[:])
-            elif c == banks - 1:
-                nc.sync.dma_start(out=out_rows[w][:, t, :], in_=product_of[(w, t)])
+                add_pass(acc, w, t, c, g)
+            finish(acc, w, t, c)
 
         def multiply_tile(w, t):
             for c in range(banks):
                 multiply(w, t, c)
 
         idle_matmuls(4)
-        half = row_tiles // 2
         for t in range(LOAD_TILES):
             flip(t)
         idle_matmuls(2)
         for t in range(LOAD_TILES, half):
             flip(t)
-        for t in range(half):
+        for t in range(half - 1):
             quantise(t)
+        first_banks = []
+        for t in range(LOAD_TILES):
+            acc = psum.tile([P, BANK], F32, tag="bank")
+            first_banks.append(acc)
+        for g in range(passes):
+            for t in range(LOAD_TILES):
+                add_pass(first_banks[t], 0, t, 0, g)
+        finish(first_banks[0], 0, 0, 0)
+        quantise(half - 1)
+        finish(first_banks[1], 0, 1, 0)
+        for t in range(LOAD_TILES):
+            multiply(0, t, 1)
+        for t in range(LOAD_TILES, half):
+            multiply_tile(0, t)
         for t in range(half, row_tiles):
             sort_words(t)
-        for c in range(banks):
-            for t in range(half - 2):
-                multiply(0, t, c)
-        multiply_tile(0, half - 2)
-        multiply(0, half - 1, 0)
+        for t in range(half - 1):
+            multiply_tile(1, t)
         for t in range(half, row_tiles):
             flip(t)
         quantise(half)
         quantise(half + 1)
-        multiply(0, half - 1, 1)
+        multiply(1, half - 1, 0)
         quantise(half + 2)
-        multiply(0, half, 0)
+        multiply(1, half - 1, 1)
         quantise(half + 3)
-        multiply(0, half, 1)
-        for t in range(half + 1, row_tiles):
-            multiply_tile(0, t)
-        for t in range(row_tiles):
-            multiply_tile(1, t)
+        for w in range(len(outs)):
+            for t in range(half, row_tiles):
+                multiply_tile(w, t)

@@ -63,8 +63,8 @@ def tile_pinnlayer_pb_kernel(
         for planes in w_planes:
             nc.vector.memset(planes[:].rearrange("p g n -> p (g n)").bitcast(I32), 0)
 
-        def load_volt(first):
-            tiles = slice(first, first + LOAD_TILES)
+        def load_volt(first, count):
+            tiles = slice(first, first + count)
             nc.sync.dma_start(out=volt[:, tiles, :], in_=volt_rows[:, tiles, :])
 
         def load_scales(w):
@@ -93,17 +93,18 @@ def tile_pinnlayer_pb_kernel(
                 .bitcast(I32),
             )
 
-        load_volt(0)
-        load_volt(2)
+        load_volt(0, 1)
+        load_volt(1, 1)
+        load_volt(2, LOAD_TILES)
         load_scales(0)
         for g in range(passes):
             load_words_of_pass(0, g, 0, BANK)
         load_words(0, BANK, BANK)
         load_scales(1)
-        load_words(1, 0, BANK)
-        load_words(1, BANK, BANK)
-        load_volt(4)
-        load_volt(6)
+        for g in range(passes):
+            load_words_of_pass(1, g, 0, width)
+        load_volt(4, LOAD_TILES)
+        load_volt(6, LOAD_TILES)
 
         def idle_matmuls(count):
             unread = psum.tile([P, BANK], F32, tag="bank")
@@ -214,13 +215,14 @@ def tile_pinnlayer_pb_kernel(
         for g in range(passes):
             for t in range(LOAD_TILES):
                 add_pass(first_banks[t], 0, t, 0, g)
-        finish(first_banks[0], 0, 0, 0)
+        for t in range(LOAD_TILES):
+            finish(first_banks[t], 0, t, 0)
+        multiply(0, LOAD_TILES, 0)
         quantise(half - 1)
-        finish(first_banks[1], 0, 1, 0)
         for t in range(LOAD_TILES):
             multiply(0, t, 1)
-        for t in range(LOAD_TILES, half):
-            multiply_tile(0, t)
+        multiply(0, LOAD_TILES, 1)
+        multiply_tile(0, half - 1)
         for t in range(half, row_tiles):
             sort_words(t)
         for t in range(half - 1):

@@ -18,6 +18,7 @@ QUADRANTS = 4
 ROWS = 4
 PLANE_FIRST = (0, 4)
 PAIRED_STORES = 3
+ALIGN = 256
 LOAD_TILES = 2
 
 FLOPS = 2 * 2 * 1024 * 1024 * 1024
@@ -48,15 +49,15 @@ def tile_pinnlayer_pb_kernel(
         psum = ctx.enter_context(tc.psum_pool(name="psum", bufs=8))
         ctx.enter_context(tc.manual_schedule())
 
-        identity = keep.tile([P, P], F32)
-        zeros = keep.tile([P, BANK], BF16)
-        volt = keep.tile([P, row_tiles, width], BF16)
-        w_words = keep.tile([P, len(outs), passes, width], U32, align_bytes=64)
-        y_planes = keep.tile([P, passes, width], U8, align_bytes=64)
-        yconj_planes = keep.tile([P, passes, width], U8, align_bytes=64)
+        identity = keep.tile([P, P], F32, align_bytes=ALIGN)
+        zeros = keep.tile([P, BANK], BF16, align_bytes=ALIGN)
+        volt = keep.tile([P, row_tiles, width], BF16, align_bytes=ALIGN)
+        w_words = keep.tile([P, len(outs), passes, width], U32, align_bytes=ALIGN)
+        y_planes = keep.tile([P, passes, width], U8, align_bytes=ALIGN)
+        yconj_planes = keep.tile([P, passes, width], U8, align_bytes=ALIGN)
         w_planes = (y_planes, yconj_planes)
-        v_words = keep.tile([P, row_tiles, passes, P], U32, align_bytes=64)
-        v_planes = keep.tile([P, row_tiles, passes, P], U8, align_bytes=64)
+        v_words = keep.tile([P, row_tiles, passes, P], U32, align_bytes=ALIGN)
+        v_planes = keep.tile([P, row_tiles, passes, P], U8, align_bytes=ALIGN)
 
         nc.vector.memset(zeros[:].bitcast(I32), 0)
         make_identity(nc, identity[:])
@@ -117,7 +118,7 @@ def tile_pinnlayer_pb_kernel(
 
         def sort_words(t):
             pairs = volt[:, t, :].bitcast(F32).rearrange("p (g j u) -> p g u j", g=passes, u=2)
-            in_order = stage.tile([P, passes, 2, P], F32)
+            in_order = stage.tile([P, passes, 2, P], F32, align_bytes=ALIGN)
             nc.scalar.copy(out=in_order[:], in_=pairs)
             sorted_of[t] = in_order
 
@@ -132,7 +133,7 @@ def tile_pinnlayer_pb_kernel(
                         first = (K_PASS // 2) * g + u
                         words = pairs[:, first : (K_PASS // 2) * (g + 1) : 2]
                     nc.tensor.transpose(flipped[:, g, u, :], words, identity[:])
-            grouped = stage.tile([P, passes, P, PACK], BF16, align_bytes=64)
+            grouped = stage.tile([P, passes, P, PACK], BF16, align_bytes=ALIGN)
             nc.scalar.copy(
                 out=grouped[:]
                 .rearrange("p g b t4 -> p (g b t4)")
@@ -156,11 +157,11 @@ def tile_pinnlayer_pb_kernel(
 
         def new_product(w, t):
             if (w, t) not in paired:
-                product = results.tile([P, width], F32)
+                product = results.tile([P, width], F32, align_bytes=ALIGN)
                 product_of[(w, t)] = product[:]
             else:
                 if t % 2 == 0:
-                    pair = pairs.tile([P, 2, width], F32)
+                    pair = pairs.tile([P, 2, width], F32, align_bytes=ALIGN)
                     pair_of[(w, t // 2)] = pair
                 product_of[(w, t)] = pair_of[(w, t // 2)][:, t % 2, :]
 

from contextlib import ExitStack

import concourse.mybir as mybir
from concourse.masks import make_identity

F32 = mybir.dt.float32
BF16 = mybir.dt.bfloat16
I32 = mybir.dt.int32
U32 = mybir.dt.uint32
U8 = mybir.dt.uint8
FP8X4 = mybir.dt.float8_e4m3fn_x4

P = 128
PACK = 4
K_PASS = P * PACK
BANK = 512
QUADRANTS = 4
ROWS = 4
PLANE_FIRST = (0, 4)
PAIRED_STORES = 3
ALIGN = 256
LOAD_TILES = 2

FLOPS = 2 * 2 * 1024 * 1024 * 1024


def tile_pinnlayer_pb_kernel(
    tc, Volt, Y_words, Y_scales, Yconj_words, Yconj_scales, out_0, out_1
):
    nc = tc.nc
    samples, width = Volt.shape
    row_tiles = samples // P
    passes = width // K_PASS
    banks = width // BANK
    words_in = (Y_words, Yconj_words)
    scales_in = (Y_scales, Yconj_scales)
    outs = (out_0, out_1)

    volt_rows = Volt.rearrange("(p t) k -> p t k", t=row_tiles)
    out_rows = [o.rearrange("(p t) n -> p t n", t=row_tiles) for o in outs]

    with ExitStack() as ctx:
        keep = ctx.enter_context(tc.tile_pool(name="keep", bufs=1))
        stage = ctx.enter_context(tc.tile_pool(name="stage", bufs=row_tiles))
        results = ctx.enter_context(
            tc.tile_pool(name="results", bufs=len(outs) * row_tiles - 2 * PAIRED_STORES)
        )
        pairs = ctx.enter_context(tc.tile_pool(name="pairs", bufs=PAIRED_STORES))
        psum = ctx.enter_context(tc.psum_pool(name="psum", bufs=8))
        ctx.enter_context(tc.manual_schedule())

        identity = keep.tile([P, P], F32, align_bytes=ALIGN)
        zeros = keep.tile([P, BANK], BF16, align_bytes=ALIGN)
        volt = keep.tile([P, row_tiles, width], BF16, align_bytes=ALIGN)
        w_words = keep.tile([P, len(outs), passes, width], U32, align_bytes=ALIGN)
        y_planes = keep.tile([P, passes, width], U8, align_bytes=ALIGN)
        yconj_planes = keep.tile([P, passes, width], U8, align_bytes=ALIGN)
        w_planes = (y_planes, yconj_planes)
        v_words = keep.tile([P, row_tiles, passes, P], U32, align_bytes=ALIGN)
        v_planes = keep.tile([P, row_tiles, passes, P], U8, align_bytes=ALIGN)

        nc.vector.memset(zeros[:].bitcast(I32), 0)
        make_identity(nc, identity[:])
        for planes in w_planes:
            nc.vector.memset(planes[:].rearrange("p g n -> p (g n)").bitcast(I32), 0)

        def load_volt(first, count):
            tiles = slice(first, first + count)
            nc.sync.dma_start(out=volt[:, tiles, :], in_=volt_rows[:, tiles, :])

        def load_scales(w):
            by_row = scales_in[w].rearrange("g q n -> q g n")
            for quadrant in range(QUADRANTS):
                first = 32 * quadrant + PLANE_FIRST[w]
                nc.sync.dma_start(
                    out=w_planes[w][first : first + ROWS, :, :].bitcast(I32),
                    in_=by_row[ROWS * quadrant : ROWS * (quadrant + 1), :, :].bitcast(I32),
                )

        def load_words(w, first, count):
            n_cols = slice(first, first + count)
            byte_cols = slice(PACK * first, PACK * (first + count))
            nc.sync.dma_start(
                out=w_words[:, w, :, n_cols].bitcast(I32),
                in_=words_in[w].rearrange("g p n t4 -> p g (n t4)")[:, :, byte_cols].bitcast(I32),
            )

        def load_words_of_pass(w, g, first, count):
            byte_cols = slice(PACK * first, PACK * (first + count))
            nc.sync.dma_start(
                out=w_words[:, w, g, first : first + count].bitcast(I32),
                in_=words_in[w][g, :, :, :]
                .rearrange("p n t4 -> p (n t4)")[:, byte_cols]
                .bitcast(I32),
            )

        load_volt(0, 1)
        load_volt(1, 1)
        load_volt(2, LOAD_TILES)
        load_scales(0)
        for g in range(passes):
            load_words_of_pass(0, g, 0, BANK)
        load_words(0, BANK, BANK)
        load_scales(1)
        for g in range(passes):
            load_words_of_pass(1, g, 0, width)
        load_volt(4, LOAD_TILES)
        load_volt(6, LOAD_TILES)

        def idle_matmuls(count):
            unread = psum.tile([P, BANK], F32, tag="bank")
            for i in range(count):
                nc.tensor.matmul(unread[:], lhsT=zeros[:, 0:P], rhs=zeros[:], start=True, stop=True)

        grouped_of = {}

        sorted_of = {}

        def sort_words(t):
            pairs = volt[:, t, :].bitcast(F32).rearrange("p (g j u) -> p g u j", g=passes, u=2)
            in_order = stage.tile([P, passes, 2, P], F32, align_bytes=ALIGN)
            nc.scalar.copy(out=in_order[:], in_=pairs)
            sorted_of[t] = in_order

        def flip(t):
            pairs = volt[:, t, :].bitcast(F32)
            flipped = psum.tile([P, passes, 2, P], F32, tag="bank")
            for g in range(passes):
                for u in range(2):
                    if t in sorted_of:
                        words = sorted_of[t][:, g, u, :]
                    else:
                        first = (K_PASS // 2) * g + u
                        words = pairs[:, first : (K_PASS // 2) * (g + 1) : 2]
                    nc.tensor.transpose(flipped[:, g, u, :], words, identity[:])
            grouped = stage.tile([P, passes, P, PACK], BF16, align_bytes=ALIGN)
            nc.scalar.copy(
                out=grouped[:]
                .rearrange("p g b t4 -> p (g b t4)")
                .bitcast(F32)
                .rearrange("p (g b u) -> p g b u", g=passes, u=2),
                in_=flipped[:].rearrange("p g u b -> p g b u"),
            )
            grouped_of[t] = grouped

        def quantise(t):
            nc.vector.quantize_mx(
                out=v_words[:, t, :, :].rearrange("p g b -> p (g b)").bitcast(FP8X4),
                scales=v_planes[:, t, :, :].rearrange("p g b -> p (g b)"),
                in_=grouped_of[t][:].rearrange("p g b t4 -> p (g b t4)"),
            )

        half = row_tiles // 2
        paired = [(w, t) for w in range(len(outs)) for t in range(half)][: 2 * PAIRED_STORES]
        pair_of = {}
        product_of = {}

        def new_product(w, t):
            if (w, t) not in paired:
                product = results.tile([P, width], F32, align_bytes=ALIGN)
                product_of[(w, t)] = product[:]
            else:
                if t % 2 == 0:
                    pair = pairs.tile([P, 2, width], F32, align_bytes=ALIGN)
                    pair_of[(w, t // 2)] = pair
                product_of[(w, t)] = pair_of[(w, t // 2)][:, t % 2, :]

        def store(w, t):
            if (w, t) not in paired:
                nc.sync.dma_start(out=out_rows[w][:, t, :], in_=product_of[(w, t)])
            elif t % 2 == 1:
                nc.sync.dma_start(out=out_rows[w][:, t - 1 : t + 1, :], in_=pair_of[(w, t // 2)][:])

        def add_pass(acc, w, t, c, g):
            n_cols = slice(BANK * c, BANK * (c + 1))
            nc.tensor.matmul_mx(
                out=acc[:],
                lhsT=v_words[:, t, g, :].bitcast(FP8X4),
                lhsT_scale=v_planes[:, t, g, :],
                rhs=w_words[:, w, g, n_cols].bitcast(FP8X4),
                rhs_scale=w_planes[w][PLANE_FIRST[w] : P, g, n_cols],
                start=(g == 0),
                stop=(g == passes - 1),
            )

        def finish(acc, w, t, c):
            if c == 0:
                new_product(w, t)
            n_cols = slice(BANK * c, BANK * (c + 1))
            nc.vector.tensor_mul(product_of[(w, t)][:, n_cols], acc[:], volt[:, t, n_cols])
            if c == banks - 1:
                store(w, t)

        def multiply(w, t, c):
            acc = psum.tile([P, BANK], F32, tag="bank")
            for g in range(passes):
                add_pass(acc, w, t, c, g)
            finish(acc, w, t, c)

        def multiply_tile(w, t):
            for c in range(banks):
                multiply(w, t, c)

        idle_matmuls(4)
        for t in range(LOAD_TILES):
            flip(t)
        idle_matmuls(2)
        for t in range(LOAD_TILES, half):
            flip(t)
        for t in range(half - 1):
            quantise(t)
        first_banks = []
        for t in range(LOAD_TILES):
            acc = psum.tile([P, BANK], F32, tag="bank")
            first_banks.append(acc)
        for g in range(passes):
            for t in range(LOAD_TILES):
                add_pass(first_banks[t], 0, t, 0, g)
        for t in range(LOAD_TILES):
            finish(first_banks[t], 0, t, 0)
        multiply(0, LOAD_TILES, 0)
        quantise(half - 1)
        for t in range(LOAD_TILES):
            multiply(0, t, 1)
        multiply(0, LOAD_TILES, 1)
        multiply_tile(0, half - 1)
        for t in range(half, row_tiles):
            sort_words(t)
        for t in range(half - 1):
            multiply_tile(1, t)
        for t in range(half, row_tiles):
            flip(t)
        quantise(half)
        quantise(half + 1)
        multiply(1, half - 1, 0)
        quantise(half + 2)
        multiply(1, half - 1, 1)
        quantise(half + 3)
        for w in range(len(outs)):
            for t in range(half, row_tiles):
                multiply_tile(w, t)
